import numpy as np
import ml_dtypes


def mxq(x, axis, fmt="e4m3"):
    dtype, down = {"e4m3": (ml_dtypes.float8_e4m3fn, 7), "e5m2": (ml_dtypes.float8_e5m2, 14)}[fmt]
    v = np.moveaxis(np.asarray(x, np.float32).astype(ml_dtypes.bfloat16).astype(np.float64), axis, -1)
    blocks = v.reshape(v.shape[:-1] + (-1, 32))
    amax = np.abs(blocks).max(-1, keepdims=True)
    byte = np.maximum(np.where(amax > 0, np.frexp(amax)[1] - 1 + 127, 0) - down, 1)
    scale = np.exp2(byte - 127.0)
    codes = (blocks / scale).astype(np.float32).astype(dtype).astype(np.float64)
    return np.moveaxis((codes * scale).reshape(v.shape), -1, axis)


WIDE = False


def mx_kscale(k):
    if not WIDE:
        return np.ones(k)
    levels = np.array([20, -20, 10, -10, 0])
    a = np.random.permutation(np.resize(levels, k // 512 * 4)).reshape(k // 512, 4)
    idx = np.arange(k)
    return np.exp2(a[idx // 512, idx % 128 // 32])


BF16 = ml_dtypes.bfloat16


def bf(x):
    return np.asarray(x, np.float32).astype(BF16)


def f64(x):
    return np.asarray(x).astype(np.float64)


B, P, L, FI, FO = 128, 2, 3, 512, 512
C = (L + 1) * (L + 1)


def setup_inputs():
    u = mx_kscale(FO)
    x = np.random.standard_normal((B, P, C, FI))
    W_e = np.random.standard_normal((L + 1, FI, FO)) / np.sqrt(FI) / u
    W_o = np.random.standard_normal((L + 1, FI, FO)) / np.sqrt(FI) / u
    b = np.random.standard_normal(FO) * 0.5
    g = np.random.standard_normal((B, P, C, FO)) * np.exp2(np.random.randint(-12, 1, (B, P, C, 1))) * 16.0 * u
    return {"x": bf(x), "W_e": bf(W_e), "W_o": bf(W_o), "b": bf(b), "grad_out": bf(g)}


def reference(x, W_e, W_o, b, grad_out):
    gq = mxq(f64(grad_out), 3, "e5m2")
    weq = mxq(f64(W_e), 2, "e4m3")
    woq = mxq(f64(W_o), 2, "e4m3")
    gs_e, gs_o = [], []
    for l in range(L + 1):
        seg = gq[:, :, l * l:(l + 1) * (l + 1), :]
        gs_e.append(seg[:, 0] @ weq[l].T)
        gs_o.append(seg[:, 1] @ woq[l].T)
    return np.stack([np.concatenate(gs_e, axis=-2), np.concatenate(gs_o, axis=-2)], axis=-3)

@@ -1,0 +1,155 @@
+from contextlib import ExitStack
+
+import concourse.masks as masks
+import concourse.mybir as mybir
+
+BF16 = mybir.dt.bfloat16
+F32 = mybir.dt.float32
+U32 = mybir.dt.uint32
+U8 = mybir.dt.uint8
+E5M2_X4 = mybir.dt.float8_e5m2_x4
+E4M3_X4 = mybir.dt.float8_e4m3fn_x4
+
+P = 128
+PARITIES = 2
+DEGREES = 4
+COMPONENTS = DEGREES * DEGREES
+FEATURES = 512
+DEGREE_OF = [degree for degree in range(DEGREES) for m in range(2 * degree + 1)]
+
+ROWS = 4
+WORDS = FEATURES // 2
+BLOCKS = WORDS // P
+ROWS_PER_BANK = 2
+BANKS = ROWS // ROWS_PER_BANK
+CHUNKS = COMPONENTS // ROWS
+
+FLOPS = 2 * P * PARITIES * COMPONENTS * FEATURES * FEATURES
+BYTES = (
+    2 * P * PARITIES * COMPONENTS * FEATURES
+    + 2 * PARITIES * DEGREES * FEATURES * FEATURES
+    + 4 * P * PARITIES * COMPONENTS * FEATURES
+)
+
+
+def components_of(chunk):
+    return range(chunk * ROWS, (chunk + 1) * ROWS)
+
+
+def degrees_first_met(chunk):
+    met_before = [DEGREE_OF[c] for c in range((chunk + 1) * ROWS, COMPONENTS)]
+    mine = sorted(set(DEGREE_OF[c] for c in components_of(chunk)), reverse=True)
+    return [degree for degree in mine if degree not in met_before]
+
+
+def tile_dense_pa_kernel(tc, x, W_e, W_o, b, grad_out, out):
+    nc = tc.nc
+    weights = [W_e, W_o]
+    work = [(parity, chunk) for parity in range(PARITIES) for chunk in reversed(range(CHUNKS))]
+
+    with ExitStack() as ctx:
+        keep = ctx.enter_context(tc.tile_pool(name="keep", bufs=1))
+        stage = ctx.enter_context(tc.tile_pool(name="stage", bufs=4))
+        flip_psum = ctx.enter_context(tc.psum_pool(name="flip_psum", bufs=4))
+        product_psum = ctx.enter_context(tc.psum_pool(name="product_psum", bufs=4))
+        ctx.enter_context(tc.manual_schedule())
+
+        identity = keep.tile([P, P], F32, name="identity")
+        masks.make_identity(nc, identity[:])
+
+        w_raw = {}
+        g_raw = {}
+        for parity, chunk in work:
+            for degree in degrees_first_met(chunk):
+                w_raw[parity, degree] = keep.tile(
+                    [P, ROWS * FEATURES], BF16, name="w_raw_%d_%d" % (parity, degree)
+                )
+                nc.sync.dma_start(
+                    out=w_raw[parity, degree][:],
+                    in_=weights[parity][degree].rearrange("(r j) k -> r (j k)", j=ROWS),
+                )
+            g_raw[parity, chunk] = keep.tile([P, ROWS * FEATURES], BF16, name="g_raw_%d_%d" % (parity, chunk))
+            first = chunk * ROWS
+            nc.sync.dma_start(
+                out=g_raw[parity, chunk][:],
+                in_=grad_out[:, parity, first : first + ROWS, :].rearrange("n c k -> n (c k)"),
+            )
+
+        def transpose_words(raw):
+            words = raw[:].bitcast(F32)
+            banks = []
+            for h in range(BANKS):
+                bank = flip_psum.tile([P, ROWS_PER_BANK * BLOCKS, P], F32, name="flipped")
+                for plane in range(ROWS_PER_BANK * BLOCKS):
+                    start = (h * ROWS_PER_BANK * BLOCKS + plane) * P
+                    nc.tensor.transpose(bank[:, plane, :], words[:, start : start + P], identity[:])
+                banks.append(bank)
+            return banks
+
+        w_codes = {}
+        w_scales = {}
+        g_codes = {}
+        g_scales = {}
+
+        def prepare(parity, chunk):
+            to_quantise = []
+            for degree in degrees_first_met(chunk):
+                banks = transpose_words(w_raw[parity, degree])
+                grouped = stage.tile([P, FEATURES * 4], BF16, name="grouped", align_bytes=64)
+                columns = grouped[:].bitcast(F32).rearrange("q (r j u) -> q r j u", j=ROWS, u=BLOCKS)
+                for h in range(BANKS):
+                    nc.vector.tensor_copy(
+                        out=columns[:, :, h * ROWS_PER_BANK : (h + 1) * ROWS_PER_BANK, :],
+                        in_=banks[h][:].rearrange("q (j u) r -> q r j u", u=BLOCKS),
+                    )
+                w_codes[parity, degree] = keep.tile(
+                    [P, FEATURES], U32, name="w_codes_%d_%d" % (parity, degree), align_bytes=64
+                )
+                w_scales[parity, degree] = keep.tile(
+                    [P, FEATURES], U8, name="w_scales_%d_%d" % (parity, degree), align_bytes=64
+                )
+                to_quantise.append((grouped, w_codes[parity, degree], w_scales[parity, degree], E4M3_X4))
+
+            banks = transpose_words(g_raw[parity, chunk])
+            grouped = stage.tile([P, ROWS * P * 4], BF16, name="grouped", align_bytes=64)
+            columns = grouped[:].bitcast(F32).rearrange("q (a n u) -> q a n u", a=ROWS, u=BLOCKS)
+            nc.vector.tensor_copy(
+                out=columns[:, 0:ROWS_PER_BANK], in_=banks[0][:].rearrange("q (a u) n -> q a n u", u=BLOCKS)
+            )
+            nc.scalar.copy(
+                out=columns[:, ROWS_PER_BANK:ROWS], in_=banks[1][:].rearrange("q (a u) n -> q a n u", u=BLOCKS)
+            )
+            g_codes[parity, chunk] = keep.tile(
+                [P, ROWS * P], U32, name="g_codes_%d_%d" % (parity, chunk), align_bytes=64
+            )
+            g_scales[parity, chunk] = keep.tile(
+                [P, ROWS * P], U8, name="g_scales_%d_%d" % (parity, chunk), align_bytes=64
+            )
+            to_quantise.append((grouped, g_codes[parity, chunk], g_scales[parity, chunk], E5M2_X4))
+
+            for grouped, codes, scales, fmt in to_quantise:
+                nc.vector.quantize_mx(out=codes[:].bitcast(fmt), scales=scales[:], in_=grouped[:])
+
+        def multiply(parity, chunk):
+            result = keep.tile([P, ROWS, FEATURES], F32, name="result_%d_%d" % (parity, chunk))
+            for a, c in enumerate(components_of(chunk)):
+                items = slice(a * P, (a + 1) * P)
+                product = product_psum.tile([P, FEATURES], F32, name="product")
+                nc.tensor.matmul_mx(
+                    out=product[:],
+                    lhsT=g_codes[parity, chunk][:, items].bitcast(E5M2_X4),
+                    lhsT_scale=g_scales[parity, chunk][:, items],
+                    rhs=w_codes[parity, DEGREE_OF[c]][:].bitcast(E4M3_X4),
+                    rhs_scale=w_scales[parity, DEGREE_OF[c]][:],
+                    start=True,
+                    stop=True,
+                )
+                nc.scalar.copy(out=result[:, a, :], in_=product[:])
+            first = chunk * ROWS
+            nc.sync.dma_start(out=out[:, parity, first : first + ROWS, :], in_=result[:])
+
+        for step, (parity, chunk) in enumerate(work):
+            prepare(parity, chunk)
+            if step > 0:
+                multiply(*work[step - 1])
+        multiply(*work[-1])

@@ -98,7 +98,7 @@ def tile_dense_pa_kernel(tc, x, W_e, W_o, b, grad_out, out):
                 grouped = stage.tile([P, FEATURES * 4], BF16, name="grouped", align_bytes=64)
                 columns = grouped[:].bitcast(F32).rearrange("q (r j u) -> q r j u", j=ROWS, u=BLOCKS)
                 for h in range(BANKS):
-                    nc.vector.tensor_copy(
+                    nc.scalar.copy(
                         out=columns[:, :, h * ROWS_PER_BANK : (h + 1) * ROWS_PER_BANK, :],
                         in_=banks[h][:].rearrange("q (j u) r -> q r j u", u=BLOCKS),
                     )
@@ -144,7 +144,10 @@ def tile_dense_pa_kernel(tc, x, W_e, W_o, b, grad_out, out):
                     start=True,
                     stop=True,
                 )
-                nc.scalar.copy(out=result[:, a, :], in_=product[:])
+                if a % 2 == 0:
+                    nc.scalar.copy(out=result[:, a, :], in_=product[:])
+                else:
+                    nc.vector.tensor_copy(out=result[:, a, :], in_=product[:])
             first = chunk * ROWS
             nc.sync.dma_start(out=out[:, parity, first : first + ROWS, :], in_=result[:])
 

@@ -23,6 +23,7 @@ BLOCKS = WORDS // P
 ROWS_PER_BANK = 2
 BANKS = ROWS // ROWS_PER_BANK
 CHUNKS = COMPONENTS // ROWS
+HALF = 2 * ROWS
 
 FLOPS = 2 * P * PARITIES * COMPONENTS * FEATURES * FEATURES
 BYTES = (
@@ -68,15 +69,16 @@ def tile_dense_pa_kernel(tc, x, W_e, W_o, b, grad_out, out):
                     out=w_raw[parity, degree][:],
                     in_=weights[parity][degree].rearrange("(r j) k -> r (j k)", j=ROWS),
                 )
-            g_raw[parity, chunk] = keep.tile([P, ROWS * FEATURES], BF16, name="g_raw_%d_%d" % (parity, chunk))
             first = chunk * ROWS
-            nc.sync.dma_start(
-                out=g_raw[parity, chunk][:],
-                in_=grad_out[:, parity, first : first + ROWS, :].rearrange("n c k -> n (c k)"),
-            )
+            if first % HALF != 0:
+                half = first // HALF
+                g_raw[parity, half] = keep.tile([P, HALF * FEATURES], BF16, name="g_raw_%d_%d" % (parity, half))
+                nc.sync.dma_start(
+                    out=g_raw[parity, half][:],
+                    in_=grad_out[:, parity, half * HALF : (half + 1) * HALF, :].rearrange("n c k -> n (c k)"),
+                )
 
-        def transpose_words(raw):
-            words = raw[:].bitcast(F32)
+        def transpose_words(words):
             banks = []
             for h in range(BANKS):
                 bank = flip_psum.tile([P, ROWS_PER_BANK * BLOCKS, P], F32, name="flipped")
@@ -90,11 +92,12 @@ def tile_dense_pa_kernel(tc, x, W_e, W_o, b, grad_out, out):
         w_scales = {}
         g_codes = {}
         g_scales = {}
+        result = {}
 
         def prepare(parity, chunk):
             to_quantise = []
             for degree in degrees_first_met(chunk):
-                banks = transpose_words(w_raw[parity, degree])
+                banks = transpose_words(w_raw[parity, degree][:].bitcast(F32))
                 grouped = stage.tile([P, FEATURES * 4], BF16, name="grouped", align_bytes=64)
                 columns = grouped[:].bitcast(F32).rearrange("q (r j u) -> q r j u", j=ROWS, u=BLOCKS)
                 for h in range(BANKS):
@@ -110,7 +113,11 @@ def tile_dense_pa_kernel(tc, x, W_e, W_o, b, grad_out, out):
                 )
                 to_quantise.append((grouped, w_codes[parity, degree], w_scales[parity, degree], E4M3_X4))
 
-            banks = transpose_words(g_raw[parity, chunk])
+            first = chunk * ROWS
+            first_word = (first % HALF) * WORDS
+            banks = transpose_words(
+                g_raw[parity, first // HALF][:].bitcast(F32)[:, first_word : first_word + ROWS * WORDS]
+            )
             grouped = stage.tile([P, ROWS * P * 4], BF16, name="grouped", align_bytes=64)
             columns = grouped[:].bitcast(F32).rearrange("q (a n u) -> q a n u", a=ROWS, u=BLOCKS)
             nc.vector.tensor_copy(
@@ -131,7 +138,10 @@ def tile_dense_pa_kernel(tc, x, W_e, W_o, b, grad_out, out):
                 nc.vector.quantize_mx(out=codes[:].bitcast(fmt), scales=scales[:], in_=grouped[:])
 
         def multiply(parity, chunk):
-            result = keep.tile([P, ROWS, FEATURES], F32, name="result_%d_%d" % (parity, chunk))
+            first = chunk * ROWS
+            half = first // HALF
+            if first % HALF != 0:
+                result[parity, half] = keep.tile([P, HALF, FEATURES], F32, name="result_%d_%d" % (parity, half))
             for a, c in enumerate(components_of(chunk)):
                 items = slice(a * P, (a + 1) * P)
                 product = product_psum.tile([P, FEATURES], F32, name="product")
@@ -145,11 +155,16 @@ def tile_dense_pa_kernel(tc, x, W_e, W_o, b, grad_out, out):
                     stop=True,
                 )
                 if a % 2 == 0:
-                    nc.scalar.copy(out=result[:, a, :], in_=product[:])
+                    nc.scalar.copy(out=result[parity, half][:, c % HALF, :], in_=product[:])
                 else:
-                    nc.vector.tensor_copy(out=result[:, a, :], in_=product[:])
-            first = chunk * ROWS
-            nc.sync.dma_start(out=out[:, parity, first : first + ROWS, :], in_=result[:])
+                    nc.vector.tensor_copy(out=result[parity, half][:, c % HALF, :], in_=product[:])
+            if (parity, half) == (PARITIES - 1, 0):
+                nc.sync.dma_start(
+                    out=out[:, parity, first : first + ROWS, :],
+                    in_=result[parity, half][:, first % HALF : first % HALF + ROWS, :],
+                )
+            elif first % HALF == 0:
+                nc.sync.dma_start(out=out[:, parity, first : first + HALF, :], in_=result[parity, half][:])
 
         for step, (parity, chunk) in enumerate(work):
             prepare(parity, chunk)

@@ -37,16 +37,12 @@ def components_of(chunk):
     return range(chunk * ROWS, (chunk + 1) * ROWS)
 
 
-def degrees_first_met(chunk):
-    met_before = [DEGREE_OF[c] for c in range((chunk + 1) * ROWS, COMPONENTS)]
-    mine = sorted(set(DEGREE_OF[c] for c in components_of(chunk)), reverse=True)
-    return [degree for degree in mine if degree not in met_before]
-
-
 def tile_dense_pa_kernel(tc, x, W_e, W_o, b, grad_out, out):
     nc = tc.nc
     weights = [W_e, W_o]
     work = [(parity, chunk) for parity in range(PARITIES) for chunk in reversed(range(CHUNKS))]
+    for chunk in range(CHUNKS):
+        assert all(DEGREE_OF[c] >= chunk for c in components_of(chunk))
 
     with ExitStack() as ctx:
         keep = ctx.enter_context(tc.tile_pool(name="keep", bufs=1))
@@ -61,14 +57,11 @@ def tile_dense_pa_kernel(tc, x, W_e, W_o, b, grad_out, out):
         w_raw = {}
         g_raw = {}
         for parity, chunk in work:
-            for degree in degrees_first_met(chunk):
-                w_raw[parity, degree] = keep.tile(
-                    [P, ROWS * FEATURES], BF16, name="w_raw_%d_%d" % (parity, degree)
-                )
-                nc.sync.dma_start(
-                    out=w_raw[parity, degree][:],
-                    in_=weights[parity][degree].rearrange("(r j) k -> r (j k)", j=ROWS),
-                )
+            w_raw[parity, chunk] = keep.tile([P, ROWS * FEATURES], BF16, name="w_raw_%d_%d" % (parity, chunk))
+            nc.sync.dma_start(
+                out=w_raw[parity, chunk][:],
+                in_=weights[parity][chunk].rearrange("(r j) k -> r (j k)", j=ROWS),
+            )
             first = chunk * ROWS
             if first % HALF != 0:
                 half = first // HALF
@@ -88,60 +81,64 @@ def tile_dense_pa_kernel(tc, x, W_e, W_o, b, grad_out, out):
                 banks.append(bank)
             return banks
 
+        w_grouped = {}
+        g_grouped = {}
         w_codes = {}
         w_scales = {}
         g_codes = {}
         g_scales = {}
         result = {}
 
-        def prepare(parity, chunk):
-            to_quantise = []
-            for degree in degrees_first_met(chunk):
-                banks = transpose_words(w_raw[parity, degree][:].bitcast(F32))
-                grouped = stage.tile([P, FEATURES * 4], BF16, name="grouped", align_bytes=64)
-                columns = grouped[:].bitcast(F32).rearrange("q (r j u) -> q r j u", j=ROWS, u=BLOCKS)
-                for h in range(BANKS):
-                    nc.scalar.copy(
-                        out=columns[:, :, h * ROWS_PER_BANK : (h + 1) * ROWS_PER_BANK, :],
-                        in_=banks[h][:].rearrange("q (j u) r -> q r j u", u=BLOCKS),
-                    )
-                w_codes[parity, degree] = keep.tile(
-                    [P, FEATURES], U32, name="w_codes_%d_%d" % (parity, degree), align_bytes=64
-                )
-                w_scales[parity, degree] = keep.tile(
-                    [P, FEATURES], U8, name="w_scales_%d_%d" % (parity, degree), align_bytes=64
-                )
-                to_quantise.append((grouped, w_codes[parity, degree], w_scales[parity, degree], E4M3_X4))
-
+        def flip(parity, chunk):
+            w_banks = transpose_words(w_raw[parity, chunk][:].bitcast(F32))
             first = chunk * ROWS
             first_word = (first % HALF) * WORDS
-            banks = transpose_words(
+            g_banks = transpose_words(
                 g_raw[parity, first // HALF][:].bitcast(F32)[:, first_word : first_word + ROWS * WORDS]
             )
-            grouped = stage.tile([P, ROWS * P * 4], BF16, name="grouped", align_bytes=64)
-            columns = grouped[:].bitcast(F32).rearrange("q (a n u) -> q a n u", a=ROWS, u=BLOCKS)
-            nc.vector.tensor_copy(
-                out=columns[:, 0:ROWS_PER_BANK], in_=banks[0][:].rearrange("q (a u) n -> q a n u", u=BLOCKS)
+            w_grouped[parity, chunk] = stage.tile([P, FEATURES * 4], BF16, name="w_grouped", align_bytes=64)
+            columns = w_grouped[parity, chunk][:].bitcast(F32).rearrange("q (r j u) -> q r j u", j=ROWS, u=BLOCKS)
+            for h in range(BANKS):
+                nc.scalar.copy(
+                    out=columns[:, :, h * ROWS_PER_BANK : (h + 1) * ROWS_PER_BANK, :],
+                    in_=w_banks[h][:].rearrange("q (j u) r -> q r j u", u=BLOCKS),
+                )
+            g_grouped[parity, chunk] = stage.tile([P, ROWS * P * 4], BF16, name="g_grouped", align_bytes=64)
+            columns = g_grouped[parity, chunk][:].bitcast(F32).rearrange("q (a n u) -> q a n u", a=ROWS, u=BLOCKS)
+            for h in range(BANKS):
+                nc.scalar.copy(
+                    out=columns[:, h * ROWS_PER_BANK : (h + 1) * ROWS_PER_BANK],
+                    in_=g_banks[h][:].rearrange("q (a u) n -> q a n u", u=BLOCKS),
+                )
+
+        def quantise_weights(parity, chunk):
+            w_codes[parity, chunk] = keep.tile(
+                [P, FEATURES], U32, name="w_codes_%d_%d" % (parity, chunk), align_bytes=64
             )
-            nc.scalar.copy(
-                out=columns[:, ROWS_PER_BANK:ROWS], in_=banks[1][:].rearrange("q (a u) n -> q a n u", u=BLOCKS)
+            w_scales[parity, chunk] = keep.tile(
+                [P, FEATURES], U8, name="w_scales_%d_%d" % (parity, chunk), align_bytes=64
             )
+            nc.vector.quantize_mx(
+                out=w_codes[parity, chunk][:].bitcast(E4M3_X4),
+                scales=w_scales[parity, chunk][:],
+                in_=w_grouped[parity, chunk][:],
+            )
+
+        def quantise_grad(parity, chunk):
             g_codes[parity, chunk] = keep.tile(
                 [P, ROWS * P], U32, name="g_codes_%d_%d" % (parity, chunk), align_bytes=64
             )
             g_scales[parity, chunk] = keep.tile(
                 [P, ROWS * P], U8, name="g_scales_%d_%d" % (parity, chunk), align_bytes=64
             )
-            to_quantise.append((grouped, g_codes[parity, chunk], g_scales[parity, chunk], E5M2_X4))
-
-            for grouped, codes, scales, fmt in to_quantise:
-                nc.vector.quantize_mx(out=codes[:].bitcast(fmt), scales=scales[:], in_=grouped[:])
+            nc.vector.quantize_mx(
+                out=g_codes[parity, chunk][:].bitcast(E5M2_X4),
+                scales=g_scales[parity, chunk][:],
+                in_=g_grouped[parity, chunk][:],
+            )
 
         def multiply(parity, chunk):
-            first = chunk * ROWS
-            half = first // HALF
-            if first % HALF != 0:
-                result[parity, half] = keep.tile([P, HALF, FEATURES], F32, name="result_%d_%d" % (parity, half))
+            products = []
             for a, c in enumerate(components_of(chunk)):
                 items = slice(a * P, (a + 1) * P)
                 product = product_psum.tile([P, FEATURES], F32, name="product")
@@ -154,10 +151,19 @@ def tile_dense_pa_kernel(tc, x, W_e, W_o, b, grad_out, out):
                     start=True,
                     stop=True,
                 )
-                if a % 2 == 0:
-                    nc.scalar.copy(out=result[parity, half][:, c % HALF, :], in_=product[:])
-                else:
-                    nc.vector.tensor_copy(out=result[parity, half][:, c % HALF, :], in_=product[:])
+                products.append(product)
+            return products
+
+        def empty(copy, parity, chunk, a, products):
+            c = chunk * ROWS + a
+            half = c // HALF
+            if (parity, half) not in result:
+                result[parity, half] = keep.tile([P, HALF, FEATURES], F32, name="result_%d_%d" % (parity, half))
+            copy(out=result[parity, half][:, c % HALF, :], in_=products[a][:])
+
+        def store(parity, chunk):
+            first = chunk * ROWS
+            half = first // HALF
             if (parity, half) == (PARITIES - 1, 0):
                 nc.sync.dma_start(
                     out=out[:, parity, first : first + ROWS, :],
@@ -166,8 +172,22 @@ def tile_dense_pa_kernel(tc, x, W_e, W_o, b, grad_out, out):
             elif first % HALF == 0:
                 nc.sync.dma_start(out=out[:, parity, first : first + HALF, :], in_=result[parity, half][:])
 
-        for step, (parity, chunk) in enumerate(work):
-            prepare(parity, chunk)
-            if step > 0:
-                multiply(*work[step - 1])
-        multiply(*work[-1])
+        for step, now in enumerate(work):
+            flip(*now)
+            quantise_weights(*now)
+            if step == 0:
+                quantise_grad(*now)
+            else:
+                before = work[step - 1]
+                products = multiply(*before)
+                empty(nc.vector.tensor_copy, before[0], before[1], 0, products)
+                quantise_grad(*now)
+                empty(nc.vector.tensor_copy, before[0], before[1], 1, products)
+                empty(nc.vector.tensor_copy, before[0], before[1], 2, products)
+                empty(nc.scalar.copy, before[0], before[1], 3, products)
+                store(*before)
+        last = work[-1]
+        products = multiply(*last)
+        for a in range(ROWS):
+            empty(nc.vector.tensor_copy if a % 2 == 0 else nc.scalar.copy, last[0], last[1], a, products)
+        store(*last)

@@ -55,7 +55,8 @@ def tile_dense_pa_kernel(tc, x, W_e, W_o, b, grad_out, out):
         masks.make_identity(nc, identity[:])
 
         w_raw = {}
-        g_raw = {}
+        g_words = {}
+        work_first_half = (work[0][0], work[0][1] * ROWS // HALF)
         for parity, chunk in work:
             w_raw[parity, chunk] = keep.tile([P, ROWS * FEATURES], BF16, name="w_raw_%d_%d" % (parity, chunk))
             nc.sync.dma_start(
@@ -63,13 +64,22 @@ def tile_dense_pa_kernel(tc, x, W_e, W_o, b, grad_out, out):
                 in_=weights[parity][chunk].rearrange("(r j) k -> r (j k)", j=ROWS),
             )
             first = chunk * ROWS
-            if first % HALF != 0:
-                half = first // HALF
-                g_raw[parity, half] = keep.tile([P, HALF * FEATURES], BF16, name="g_raw_%d_%d" % (parity, half))
+            half = first // HALF
+            if (parity, half) == work_first_half:
+                piece = keep.tile([P, ROWS * FEATURES], BF16, name="g_raw_%d_%d_%d" % (parity, half, chunk))
                 nc.sync.dma_start(
-                    out=g_raw[parity, half][:],
+                    out=piece[:],
+                    in_=grad_out[:, parity, first : first + ROWS, :].rearrange("n c k -> n (c k)"),
+                )
+                g_words[parity, chunk] = piece[:].bitcast(F32)
+            elif first % HALF != 0:
+                piece = keep.tile([P, HALF * FEATURES], BF16, name="g_raw_%d_%d" % (parity, half))
+                nc.sync.dma_start(
+                    out=piece[:],
                     in_=grad_out[:, parity, half * HALF : (half + 1) * HALF, :].rearrange("n c k -> n (c k)"),
                 )
+                g_words[parity, chunk - 1] = piece[:].bitcast(F32)[:, 0 : ROWS * WORDS]
+                g_words[parity, chunk] = piece[:].bitcast(F32)[:, ROWS * WORDS : HALF * WORDS]
 
         def transpose_words(words):
             banks = []
@@ -91,11 +101,7 @@ def tile_dense_pa_kernel(tc, x, W_e, W_o, b, grad_out, out):
 
         def flip(parity, chunk):
             w_banks = transpose_words(w_raw[parity, chunk][:].bitcast(F32))
-            first = chunk * ROWS
-            first_word = (first % HALF) * WORDS
-            g_banks = transpose_words(
-                g_raw[parity, first // HALF][:].bitcast(F32)[:, first_word : first_word + ROWS * WORDS]
-            )
+            g_banks = transpose_words(g_words[parity, chunk])
             w_grouped[parity, chunk] = stage.tile([P, FEATURES * 4], BF16, name="w_grouped", align_bytes=64)
             columns = w_grouped[parity, chunk][:].bitcast(F32).rearrange("q (r j u) -> q r j u", j=ROWS, u=BLOCKS)
             for h in range(BANKS):

@@ -196,4 +196,9 @@ def tile_dense_pa_kernel(tc, x, W_e, W_o, b, grad_out, out):
         products = multiply(*last)
         for a in range(ROWS):
             empty(nc.vector.tensor_copy if a % 2 == 0 else nc.scalar.copy, last[0], last[1], a, products)
-        store(*last)
+            if a % 2 == 1:
+                c = last[1] * ROWS + a
+                nc.sync.dma_start(
+                    out=out[:, last[0], c - 1 : c + 1, :],
+                    in_=result[last[0], c // HALF][:, c % HALF - 1 : c % HALF + 1, :],
+                )

@@ -58,7 +58,9 @@ def tile_dense_pa_kernel(tc, x, W_e, W_o, b, grad_out, out):
         g_words = {}
         work_first_half = (work[0][0], work[0][1] * ROWS // HALF)
         for parity, chunk in work:
-            w_raw[parity, chunk] = keep.tile([P, ROWS * FEATURES], BF16, name="w_raw_%d_%d" % (parity, chunk))
+            w_raw[parity, chunk] = keep.tile(
+                [P, ROWS * FEATURES], BF16, name="w_raw_%d_%d" % (parity, chunk), align_bytes=256
+            )
             nc.sync.dma_start(
                 out=w_raw[parity, chunk][:],
                 in_=weights[parity][chunk].rearrange("(r j) k -> r (j k)", j=ROWS),
@@ -66,14 +68,16 @@ def tile_dense_pa_kernel(tc, x, W_e, W_o, b, grad_out, out):
             first = chunk * ROWS
             half = first // HALF
             if (parity, half) == work_first_half:
-                piece = keep.tile([P, ROWS * FEATURES], BF16, name="g_raw_%d_%d_%d" % (parity, half, chunk))
+                piece = keep.tile(
+                    [P, ROWS * FEATURES], BF16, name="g_raw_%d_%d_%d" % (parity, half, chunk), align_bytes=256
+                )
                 nc.sync.dma_start(
                     out=piece[:],
                     in_=grad_out[:, parity, first : first + ROWS, :].rearrange("n c k -> n (c k)"),
                 )
                 g_words[parity, chunk] = piece[:].bitcast(F32)
             elif first % HALF != 0:
-                piece = keep.tile([P, HALF * FEATURES], BF16, name="g_raw_%d_%d" % (parity, half))
+                piece = keep.tile([P, HALF * FEATURES], BF16, name="g_raw_%d_%d" % (parity, half), align_bytes=256)
                 nc.sync.dma_start(
                     out=piece[:],
                     in_=grad_out[:, parity, half * HALF : (half + 1) * HALF, :].rearrange("n c k -> n (c k)"),
@@ -164,7 +168,9 @@ def tile_dense_pa_kernel(tc, x, W_e, W_o, b, grad_out, out):
             c = chunk * ROWS + a
             half = c // HALF
             if (parity, half) not in result:
-                result[parity, half] = keep.tile([P, HALF, FEATURES], F32, name="result_%d_%d" % (parity, half))
+                result[parity, half] = keep.tile(
+                    [P, HALF, FEATURES], F32, name="result_%d_%d" % (parity, half), align_bytes=256
+                )
             copy(out=result[parity, half][:, c % HALF, :], in_=products[a][:])
 
         def store(parity, chunk):

from contextlib import ExitStack

import concourse.masks as masks
import concourse.mybir as mybir

BF16 = mybir.dt.bfloat16
F32 = mybir.dt.float32
U32 = mybir.dt.uint32
U8 = mybir.dt.uint8
E5M2_X4 = mybir.dt.float8_e5m2_x4
E4M3_X4 = mybir.dt.float8_e4m3fn_x4

P = 128
PARITIES = 2
DEGREES = 4
COMPONENTS = DEGREES * DEGREES
FEATURES = 512
DEGREE_OF = [degree for degree in range(DEGREES) for m in range(2 * degree + 1)]

ROWS = 4
WORDS = FEATURES // 2
BLOCKS = WORDS // P
ROWS_PER_BANK = 2
BANKS = ROWS // ROWS_PER_BANK
CHUNKS = COMPONENTS // ROWS
HALF = 2 * ROWS

FLOPS = 2 * P * PARITIES * COMPONENTS * FEATURES * FEATURES
BYTES = (
    2 * P * PARITIES * COMPONENTS * FEATURES
    + 2 * PARITIES * DEGREES * FEATURES * FEATURES
    + 4 * P * PARITIES * COMPONENTS * FEATURES
)


def components_of(chunk):
    return range(chunk * ROWS, (chunk + 1) * ROWS)


def tile_dense_pa_kernel(tc, x, W_e, W_o, b, grad_out, out):
    nc = tc.nc
    weights = [W_e, W_o]
    work = [(parity, chunk) for parity in range(PARITIES) for chunk in reversed(range(CHUNKS))]
    for chunk in range(CHUNKS):
        assert all(DEGREE_OF[c] >= chunk for c in components_of(chunk))

    with ExitStack() as ctx:
        keep = ctx.enter_context(tc.tile_pool(name="keep", bufs=1))
        stage = ctx.enter_context(tc.tile_pool(name="stage", bufs=4))
        flip_psum = ctx.enter_context(tc.psum_pool(name="flip_psum", bufs=4))
        product_psum = ctx.enter_context(tc.psum_pool(name="product_psum", bufs=4))
        ctx.enter_context(tc.manual_schedule())

        identity = keep.tile([P, P], F32, name="identity")
        masks.make_identity(nc, identity[:])

        w_raw = {}
        g_words = {}
        work_first_half = (work[0][0], work[0][1] * ROWS // HALF)
        for parity, chunk in work:
            w_raw[parity, chunk] = keep.tile(
                [P, ROWS * FEATURES], BF16, name="w_raw_%d_%d" % (parity, chunk), align_bytes=256
            )
            nc.sync.dma_start(
                out=w_raw[parity, chunk][:],
                in_=weights[parity][chunk].rearrange("(r j) k -> r (j k)", j=ROWS),
            )
            first = chunk * ROWS
            half = first // HALF
            if (parity, half) == work_first_half:
                piece = keep.tile(
                    [P, ROWS * FEATURES], BF16, name="g_raw_%d_%d_%d" % (parity, half, chunk), align_bytes=256
                )
                nc.sync.dma_start(
                    out=piece[:],
                    in_=grad_out[:, parity, first : first + ROWS, :].rearrange("n c k -> n (c k)"),
                )
                g_words[parity, chunk] = piece[:].bitcast(F32)
            elif first % HALF != 0:
                piece = keep.tile([P, HALF * FEATURES], BF16, name="g_raw_%d_%d" % (parity, half), align_bytes=256)
                nc.sync.dma_start(
                    out=piece[:],
                    in_=grad_out[:, parity, half * HALF : (half + 1) * HALF, :].rearrange("n c k -> n (c k)"),
                )
                g_words[parity, chunk - 1] = piece[:].bitcast(F32)[:, 0 : ROWS * WORDS]
                g_words[parity, chunk] = piece[:].bitcast(F32)[:, ROWS * WORDS : HALF * WORDS]

        def transpose_words(words):
            banks = []
            for h in range(BANKS):
                bank = flip_psum.tile([P, ROWS_PER_BANK * BLOCKS, P], F32, name="flipped")
                for plane in range(ROWS_PER_BANK * BLOCKS):
                    start = (h * ROWS_PER_BANK * BLOCKS + plane) * P
                    nc.tensor.transpose(bank[:, plane, :], words[:, start : start + P], identity[:])
                banks.append(bank)
            return banks

        w_grouped = {}
        g_grouped = {}
        w_codes = {}
        w_scales = {}
        g_codes = {}
        g_scales = {}
        result = {}

        def flip(parity, chunk):
            w_banks = transpose_words(w_raw[parity, chunk][:].bitcast(F32))
            g_banks = transpose_words(g_words[parity, chunk])
            w_grouped[parity, chunk] = stage.tile([P, FEATURES * 4], BF16, name="w_grouped", align_bytes=64)
            columns = w_grouped[parity, chunk][:].bitcast(F32).rearrange("q (r j u) -> q r j u", j=ROWS, u=BLOCKS)
            for h in range(BANKS):
                nc.scalar.copy(
                    out=columns[:, :, h * ROWS_PER_BANK : (h + 1) * ROWS_PER_BANK, :],
                    in_=w_banks[h][:].rearrange("q (j u) r -> q r j u", u=BLOCKS),
                )
            g_grouped[parity, chunk] = stage.tile([P, ROWS * P * 4], BF16, name="g_grouped", align_bytes=64)
            columns = g_grouped[parity, chunk][:].bitcast(F32).rearrange("q (a n u) -> q a n u", a=ROWS, u=BLOCKS)
            for h in range(BANKS):
                nc.scalar.copy(
                    out=columns[:, h * ROWS_PER_BANK : (h + 1) * ROWS_PER_BANK],
                    in_=g_banks[h][:].rearrange("q (a u) n -> q a n u", u=BLOCKS),
                )

        def quantise_weights(parity, chunk):
            w_codes[parity, chunk] = keep.tile(
                [P, FEATURES], U32, name="w_codes_%d_%d" % (parity, chunk), align_bytes=64
            )
            w_scales[parity, chunk] = keep.tile(
                [P, FEATURES], U8, name="w_scales_%d_%d" % (parity, chunk), align_bytes=64
            )
            nc.vector.quantize_mx(
                out=w_codes[parity, chunk][:].bitcast(E4M3_X4),
                scales=w_scales[parity, chunk][:],
                in_=w_grouped[parity, chunk][:],
            )

        def quantise_grad(parity, chunk):
            g_codes[parity, chunk] = keep.tile(
                [P, ROWS * P], U32, name="g_codes_%d_%d" % (parity, chunk), align_bytes=64
            )
            g_scales[parity, chunk] = keep.tile(
                [P, ROWS * P], U8, name="g_scales_%d_%d" % (parity, chunk), align_bytes=64
            )
            nc.vector.quantize_mx(
                out=g_codes[parity, chunk][:].bitcast(E5M2_X4),
                scales=g_scales[parity, chunk][:],
                in_=g_grouped[parity, chunk][:],
            )

        def multiply(parity, chunk):
            products = []
            for a, c in enumerate(components_of(chunk)):
                items = slice(a * P, (a + 1) * P)
                product = product_psum.tile([P, FEATURES], F32, name="product")
                nc.tensor.matmul_mx(
                    out=product[:],
                    lhsT=g_codes[parity, chunk][:, items].bitcast(E5M2_X4),
                    lhsT_scale=g_scales[parity, chunk][:, items],
                    rhs=w_codes[parity, DEGREE_OF[c]][:].bitcast(E4M3_X4),
                    rhs_scale=w_scales[parity, DEGREE_OF[c]][:],
                    start=True,
                    stop=True,
                )
                products.append(product)
            return products

        def empty(copy, parity, chunk, a, products):
            c = chunk * ROWS + a
            half = c // HALF
            if (parity, half) not in result:
                result[parity, half] = keep.tile(
                    [P, HALF, FEATURES], F32, name="result_%d_%d" % (parity, half), align_bytes=256
                )
            copy(out=result[parity, half][:, c % HALF, :], in_=products[a][:])

        def store(parity, chunk):
            first = chunk * ROWS
            half = first // HALF
            if (parity, half) == (PARITIES - 1, 0):
                nc.sync.dma_start(
                    out=out[:, parity, first : first + ROWS, :],
                    in_=result[parity, half][:, first % HALF : first % HALF + ROWS, :],
                )
            elif first % HALF == 0:
                nc.sync.dma_start(out=out[:, parity, first : first + HALF, :], in_=result[parity, half][:])

        for step, now in enumerate(work):
            flip(*now)
            quantise_weights(*now)
            if step == 0:
                quantise_grad(*now)
            else:
                before = work[step - 1]
                products = multiply(*before)
                empty(nc.vector.tensor_copy, before[0], before[1], 0, products)
                quantise_grad(*now)
                empty(nc.vector.tensor_copy, before[0], before[1], 1, products)
                empty(nc.vector.tensor_copy, before[0], before[1], 2, products)
                empty(nc.scalar.copy, before[0], before[1], 3, products)
                store(*before)
        last = work[-1]
        products = multiply(*last)
        for a in range(ROWS):
            empty(nc.vector.tensor_copy if a % 2 == 0 else nc.scalar.copy, last[0], last[1], a, products)
            if a % 2 == 1:
                c = last[1] * ROWS + a
                nc.sync.dma_start(
                    out=out[:, last[0], c - 1 : c + 1, :],
                    in_=result[last[0], c // HALF][:, c % HALF - 1 : c % HALF + 1, :],
                )
